import numpy as np
import ml_dtypes

BF16 = ml_dtypes.bfloat16


def bf(x):
    return np.asarray(x, np.float32).astype(BF16)


def f32(x):
    return np.asarray(x, np.float32)


def f64(x):
    return np.asarray(x).astype(np.float64)


def striped(idx):
    return np.tile(idx.reshape(-1, 16).T, (8, 1))


V, D, A, NC, N = 256, 128, 256, 128, 512


def elu(v):
    return np.maximum(v, 0.0) + np.exp(np.minimum(v, 0.0)) - 1.0


def setup_inputs():
    return {"table": bf(np.random.standard_normal((D, V))), "w": bf(np.random.standard_normal((D, A)) / np.sqrt(D)), "b": f32(0.1 * np.random.standard_normal((A, 1))), "lv_w": bf(np.random.standard_normal((A, A)) / np.sqrt(A)), "lv_b": f32(0.1 * np.random.standard_normal((A, 1))), "cls_w": bf(np.random.standard_normal((A, NC)) / np.sqrt(A)), "cls_b": f32(0.1 * np.random.standard_normal((NC, 1))), "offs": striped(np.random.permutation(np.tile(np.arange(V), 2))[:N])}


def reference(table, w, b, lv_w, lv_b, cls_w, cls_b, offs):
    idx = offs[:16].T.reshape(-1)
    h1 = elu(f64(w).T @ f64(table)[:, idx] + f64(b))
    h2 = elu(f64(lv_w).T @ h1 + f64(lv_b))
    return f64(cls_w).T @ h2 + f64(cls_b)

@@ -1,0 +1,77 @@
+import concourse.mybir as mybir
+
+BF16, F32, U16 = mybir.dt.bfloat16, mybir.dt.float32, mybir.dt.uint16
+ADD, MIN, MAX = mybir.AluOpType.add, mybir.AluOpType.min, mybir.AluOpType.max
+EXP, IDENTITY = mybir.ActivationFunctionType.Exp, mybir.ActivationFunctionType.Identity
+
+P = 128
+V = 256
+A = 256
+BLOCKS = A // P
+N = 512
+PIECE = 256
+PIECES = N // PIECE
+
+FLOPS = 2 * N * (P * A + A * A + A * P)
+
+
+def elu_bf16(nc, work, h, acc, bias):
+    e = work.tile([P, PIECE], F32, name="e")
+    nc.scalar.activation(e[:], acc[:], EXP, bias=bias)
+    t = work.tile([P, PIECE], F32, name="t")
+    nc.vector.tensor_scalar(t[:], e[:], -1.0, 0.0, ADD, MIN)
+    nc.vector.scalar_tensor_tensor(h[:], acc[:], bias, t[:], ADD, MAX)
+
+
+def tile_hisan_kernel(tc, table, w, b, lv_w, lv_b, cls_w, cls_b, offs, out):
+    nc = tc.nc
+    with (
+        tc.tile_pool(name="held", bufs=1) as held,
+        tc.tile_pool(name="work", bufs=4) as work,
+        tc.psum_pool(name="psum", bufs=8) as psum,
+    ):
+        offsets = held.tile([P, N // 16], U16, name="offsets")
+        nc.sync.dma_start(offsets[:], offs)
+        table_sb = held.tile([P, V], BF16, name="table_sb")
+        nc.sync.dma_start(table_sb[:], table)
+        w_sb = held.tile([P, A], BF16, name="w_sb")
+        nc.scalar.dma_start(w_sb[:], w)
+        lv_w_sb = held.tile([P, BLOCKS, A], BF16, name="lv_w_sb")
+        nc.sync.dma_start(lv_w_sb[:], lv_w.rearrange("(k p) c -> p k c", p=P))
+        cls_w_sb = held.tile([P, BLOCKS, P], BF16, name="cls_w_sb")
+        nc.sync.dma_start(cls_w_sb[:], cls_w.rearrange("(k p) m -> p k m", p=P))
+        b_sb = held.tile([P, BLOCKS], F32, name="b_sb")
+        lv_b_sb = held.tile([P, BLOCKS], F32, name="lv_b_sb")
+        cls_b_sb = held.tile([P, 1], F32, name="cls_b_sb")
+        with nc.allow_non_contiguous_dma(reason="a bias goes one element to a partition"):
+            nc.scalar.dma_start(b_sb[:], b.rearrange("(k p) o -> p (k o)", p=P))
+            nc.scalar.dma_start(lv_b_sb[:], lv_b.rearrange("(k p) o -> p (k o)", p=P))
+            nc.scalar.dma_start(cls_b_sb[:], cls_b)
+
+
+        h1 = [[held.tile([P, PIECE], BF16, name=f"h1_{p}_{k}") for k in range(BLOCKS)] for p in range(PIECES)]
+        for p in range(PIECES):
+            looked_up = table_sb[:].indirect(offsets[:, p * (PIECE // 16) : (p + 1) * (PIECE // 16)])
+            for k in range(BLOCKS):
+                acc = psum.tile([P, PIECE], F32, name="acc")
+                nc.tensor.matmul(acc[:], w_sb[:, k * P : (k + 1) * P], looked_up, start=True, stop=True)
+                elu_bf16(nc, work, h1[p][k], acc, b_sb[:, k : k + 1])
+
+        h2 = [[held.tile([P, PIECE], BF16, name=f"h2_{p}_{c}") for c in range(BLOCKS)] for p in range(PIECES)]
+        for p in range(PIECES):
+            for c in range(BLOCKS):
+                acc = psum.tile([P, PIECE], F32, name="acc")
+                for k in range(BLOCKS):
+                    nc.tensor.matmul(
+                        acc[:], lv_w_sb[:, k, c * P : (c + 1) * P], h1[p][k][:],
+                        start=(k == 0), stop=(k == BLOCKS - 1),
+                    )
+                elu_bf16(nc, work, h2[p][c], acc, lv_b_sb[:, c : c + 1])
+
+        for p in range(PIECES):
+            acc = psum.tile([P, PIECE], F32, name="acc")
+            for c in range(BLOCKS):
+                nc.tensor.matmul(acc[:], cls_w_sb[:, c, :], h2[p][c][:], start=(c == 0), stop=(c == BLOCKS - 1))
+            logits = work.tile([P, PIECE], F32, name="logits")
+            nc.scalar.activation(logits[:], acc[:], IDENTITY, bias=cls_b_sb[:, 0:1])
+            nc.sync.dma_start(out[:, p * PIECE : (p + 1) * PIECE], logits[:])

@@ -31,22 +31,27 @@ def tile_hisan_kernel(tc, table, w, b, lv_w, lv_b, cls_w, cls_b, offs, out):
         tc.psum_pool(name="psum", bufs=8) as psum,
     ):
         offsets = held.tile([P, N // 16], U16, name="offsets")
-        nc.sync.dma_start(offsets[:], offs)
         table_sb = held.tile([P, V], BF16, name="table_sb")
-        nc.sync.dma_start(table_sb[:], table)
         w_sb = held.tile([P, A], BF16, name="w_sb")
-        nc.scalar.dma_start(w_sb[:], w)
-        lv_w_sb = held.tile([P, BLOCKS, A], BF16, name="lv_w_sb")
-        nc.sync.dma_start(lv_w_sb[:], lv_w.rearrange("(k p) c -> p k c", p=P))
-        cls_w_sb = held.tile([P, BLOCKS, P], BF16, name="cls_w_sb")
-        nc.sync.dma_start(cls_w_sb[:], cls_w.rearrange("(k p) m -> p k m", p=P))
         b_sb = held.tile([P, BLOCKS], F32, name="b_sb")
+        lv_w_sb = held.tile([P, BLOCKS, A], BF16, name="lv_w_sb")
         lv_b_sb = held.tile([P, BLOCKS], F32, name="lv_b_sb")
+        cls_w_sb = held.tile([P, BLOCKS, P], BF16, name="cls_w_sb")
         cls_b_sb = held.tile([P, 1], F32, name="cls_b_sb")
         with nc.allow_non_contiguous_dma(reason="a bias goes one element to a partition"):
+            nc.sync.dma_start(offsets[:], offs)
+            nc.sync.dma_start(table_sb[:], table)
+            nc.scalar.dma_start(w_sb[:], w)
             nc.scalar.dma_start(b_sb[:], b.rearrange("(k p) o -> p (k o)", p=P))
-            nc.scalar.dma_start(lv_b_sb[:], lv_b.rearrange("(k p) o -> p (k o)", p=P))
-            nc.scalar.dma_start(cls_b_sb[:], cls_b)
+            nc.sync.dma_start(lv_w_sb[:], lv_w.rearrange("(k p) c -> p k c", p=P))
+            nc.sync.dma_start(lv_b_sb[:], lv_b.rearrange("(k p) o -> p (k o)", p=P))
+            nc.sync.dma_start(cls_w_sb[:], cls_w.rearrange("(k p) m -> p k m", p=P))
+            nc.sync.dma_start(cls_b_sb[:], cls_b)
+
+        zero = held.tile([P, 1], F32, name="zero")
+        nc.vector.memset(zero[:], 0.0)
+        one = held.tile([P, 1], F32, name="one")
+        nc.scalar.activation(one[:], zero[:], EXP)
 
 
         h1 = [[held.tile([P, PIECE], BF16, name=f"h1_{p}_{k}") for k in range(BLOCKS)] for p in range(PIECES)]

@@ -11,6 +11,7 @@ BLOCKS = A // P
 N = 512
 PIECE = 256
 PIECES = N // PIECE
+WARM_MATMULS = 8
 
 FLOPS = 2 * N * (P * A + A * A + A * P)
 
@@ -28,7 +29,8 @@ def tile_hisan_kernel(tc, table, w, b, lv_w, lv_b, cls_w, cls_b, offs, out):
     with (
         tc.tile_pool(name="held", bufs=1) as held,
         tc.tile_pool(name="work", bufs=4) as work,
-        tc.psum_pool(name="psum", bufs=8) as psum,
+        tc.psum_pool(name="psum", bufs=7) as psum,
+        tc.psum_pool(name="warm", bufs=1) as warm,
     ):
         offsets = held.tile([P, N // 16], U16, name="offsets")
         table_sb = held.tile([P, V], BF16, name="table_sb")
@@ -52,6 +54,12 @@ def tile_hisan_kernel(tc, table, w, b, lv_w, lv_b, cls_w, cls_b, offs, out):
         nc.vector.memset(zero[:], 0.0)
         one = held.tile([P, 1], F32, name="one")
         nc.scalar.activation(one[:], zero[:], EXP)
+
+        zeros = held.tile([P, PIECE], BF16, name="zeros")
+        nc.vector.memset(zeros[:], 0.0)
+        unread = warm.tile([P, PIECE], F32, name="unread")
+        for i in range(WARM_MATMULS):
+            nc.tensor.matmul(unread[:], zeros[:, 0:P], zeros[:], start=True, stop=True)
 
 
         h1 = [[held.tile([P, PIECE], BF16, name=f"h1_{p}_{k}") for k in range(BLOCKS)] for p in range(PIECES)]

@@ -9,9 +9,8 @@ V = 256
 A = 256
 BLOCKS = A // P
 N = 512
-PIECE = 256
+PIECE = 128
 PIECES = N // PIECE
-WARM_MATMULS = 8
 
 FLOPS = 2 * N * (P * A + A * A + A * P)
 
@@ -28,9 +27,8 @@ def tile_hisan_kernel(tc, table, w, b, lv_w, lv_b, cls_w, cls_b, offs, out):
     nc = tc.nc
     with (
         tc.tile_pool(name="held", bufs=1) as held,
-        tc.tile_pool(name="work", bufs=4) as work,
-        tc.psum_pool(name="psum", bufs=7) as psum,
-        tc.psum_pool(name="warm", bufs=1) as warm,
+        tc.tile_pool(name="work", bufs=8) as work,
+        tc.psum_pool(name="psum", bufs=8) as psum,
     ):
         offsets = held.tile([P, N // 16], U16, name="offsets")
         table_sb = held.tile([P, V], BF16, name="table_sb")
@@ -54,12 +52,6 @@ def tile_hisan_kernel(tc, table, w, b, lv_w, lv_b, cls_w, cls_b, offs, out):
         nc.vector.memset(zero[:], 0.0)
         one = held.tile([P, 1], F32, name="one")
         nc.scalar.activation(one[:], zero[:], EXP)
-
-        zeros = held.tile([P, PIECE], BF16, name="zeros")
-        nc.vector.memset(zeros[:], 0.0)
-        unread = warm.tile([P, PIECE], F32, name="unread")
-        for i in range(WARM_MATMULS):
-            nc.tensor.matmul(unread[:], zeros[:, 0:P], zeros[:], start=True, stop=True)
 
 
         h1 = [[held.tile([P, PIECE], BF16, name=f"h1_{p}_{k}") for k in range(BLOCKS)] for p in range(PIECES)]

@@ -11,25 +11,32 @@ BLOCKS = A // P
 N = 512
 PIECE = 128
 PIECES = N // PIECE
+WARM_MATMULS = 14
 
 FLOPS = 2 * N * (P * A + A * A + A * P)
 
 
 def elu_bf16(nc, work, h, acc, bias):
-    e = work.tile([P, PIECE], F32, name="e")
-    nc.scalar.activation(e[:], acc[:], EXP, bias=bias)
-    t = work.tile([P, PIECE], F32, name="t")
+    e = work.tile([P, BLOCKS, PIECE], F32, name="e")
+    for k in range(BLOCKS):
+        nc.scalar.activation(e[:, k, :], acc[:, k, :], EXP, bias=bias[:, k : k + 1])
+    t = work.tile([P, BLOCKS, PIECE], F32, name="t")
     nc.vector.tensor_scalar(t[:], e[:], -1.0, 0.0, ADD, MIN)
-    nc.vector.scalar_tensor_tensor(h[:], acc[:], bias, t[:], ADD, MAX)
+    for k in range(BLOCKS):
+        nc.vector.scalar_tensor_tensor(h[:, k, :], acc[:, k, :], bias[:, k : k + 1], t[:, k, :], ADD, MAX)
 
 
 def tile_hisan_kernel(tc, table, w, b, lv_w, lv_b, cls_w, cls_b, offs, out):
     nc = tc.nc
     with (
         tc.tile_pool(name="held", bufs=1) as held,
-        tc.tile_pool(name="work", bufs=8) as work,
-        tc.psum_pool(name="psum", bufs=8) as psum,
+        tc.tile_pool(name="work", bufs=4) as work,
+        tc.psum_pool(name="warm", bufs=1) as warm,
+        tc.psum_pool(name="psum", bufs=7) as psum,
     ):
+        zeros = held.tile([P, P], BF16, name="zeros")
+        nc.vector.memset(zeros[:], 0.0)
+
         offsets = held.tile([P, N // 16], U16, name="offsets")
         table_sb = held.tile([P, V], BF16, name="table_sb")
         w_sb = held.tile([P, A], BF16, name="w_sb")
@@ -48,35 +55,37 @@ def tile_hisan_kernel(tc, table, w, b, lv_w, lv_b, cls_w, cls_b, offs, out):
             nc.sync.dma_start(cls_w_sb[:], cls_w.rearrange("(k p) m -> p k m", p=P))
             nc.sync.dma_start(cls_b_sb[:], cls_b)
 
-        zero = held.tile([P, 1], F32, name="zero")
-        nc.vector.memset(zero[:], 0.0)
         one = held.tile([P, 1], F32, name="one")
-        nc.scalar.activation(one[:], zero[:], EXP)
+        nc.scalar.activation(one[:], zeros[:, 0:1], EXP)
+
+        unread = warm.tile([P, P], F32, name="unread")
+        for i in range(WARM_MATMULS):
+            nc.tensor.matmul(unread[:], zeros[:], zeros[:], start=True, stop=True)
 
 
-        h1 = [[held.tile([P, PIECE], BF16, name=f"h1_{p}_{k}") for k in range(BLOCKS)] for p in range(PIECES)]
+        h1 = [held.tile([P, BLOCKS, PIECE], BF16, name=f"h1_{p}") for p in range(PIECES)]
         for p in range(PIECES):
             looked_up = table_sb[:].indirect(offsets[:, p * (PIECE // 16) : (p + 1) * (PIECE // 16)])
+            acc = psum.tile([P, BLOCKS, PIECE], F32, name="acc")
             for k in range(BLOCKS):
-                acc = psum.tile([P, PIECE], F32, name="acc")
-                nc.tensor.matmul(acc[:], w_sb[:, k * P : (k + 1) * P], looked_up, start=True, stop=True)
-                elu_bf16(nc, work, h1[p][k], acc, b_sb[:, k : k + 1])
+                nc.tensor.matmul(acc[:, k, :], w_sb[:, k * P : (k + 1) * P], looked_up, start=True, stop=True)
+            elu_bf16(nc, work, h1[p], acc, b_sb)
 
-        h2 = [[held.tile([P, PIECE], BF16, name=f"h2_{p}_{c}") for c in range(BLOCKS)] for p in range(PIECES)]
+        h2 = [held.tile([P, BLOCKS, PIECE], BF16, name=f"h2_{p}") for p in range(PIECES)]
         for p in range(PIECES):
+            acc = psum.tile([P, BLOCKS, PIECE], F32, name="acc")
             for c in range(BLOCKS):
-                acc = psum.tile([P, PIECE], F32, name="acc")
                 for k in range(BLOCKS):
                     nc.tensor.matmul(
-                        acc[:], lv_w_sb[:, k, c * P : (c + 1) * P], h1[p][k][:],
+                        acc[:, c, :], lv_w_sb[:, k, c * P : (c + 1) * P], h1[p][:, k, :],
                         start=(k == 0), stop=(k == BLOCKS - 1),
                     )
-                elu_bf16(nc, work, h2[p][c], acc, lv_b_sb[:, c : c + 1])
+            elu_bf16(nc, work, h2[p], acc, lv_b_sb)
 
         for p in range(PIECES):
             acc = psum.tile([P, PIECE], F32, name="acc")
             for c in range(BLOCKS):
-                nc.tensor.matmul(acc[:], cls_w_sb[:, c, :], h2[p][c][:], start=(c == 0), stop=(c == BLOCKS - 1))
+                nc.tensor.matmul(acc[:], cls_w_sb[:, c, :], h2[p][:, c, :], start=(c == 0), stop=(c == BLOCKS - 1))
             logits = work.tile([P, PIECE], F32, name="logits")
             nc.scalar.activation(logits[:], acc[:], IDENTITY, bias=cls_b_sb[:, 0:1])
             nc.sync.dma_start(out[:, p * PIECE : (p + 1) * PIECE], logits[:])

@@ -17,22 +17,20 @@ FLOPS = 2 * N * (P * A + A * A + A * P)
 
 
 def elu_bf16(nc, work, h, acc, bias):
-    e = work.tile([P, BLOCKS, PIECE], F32, name="e")
-    for k in range(BLOCKS):
-        nc.scalar.activation(e[:, k, :], acc[:, k, :], EXP, bias=bias[:, k : k + 1])
-    t = work.tile([P, BLOCKS, PIECE], F32, name="t")
+    e = work.tile([P, PIECE], F32, name="e")
+    nc.scalar.activation(e[:], acc[:], EXP, bias=bias)
+    t = work.tile([P, PIECE], F32, name="t")
     nc.vector.tensor_scalar(t[:], e[:], -1.0, 0.0, ADD, MIN)
-    for k in range(BLOCKS):
-        nc.vector.scalar_tensor_tensor(h[:, k, :], acc[:, k, :], bias[:, k : k + 1], t[:, k, :], ADD, MAX)
+    nc.vector.scalar_tensor_tensor(h[:], acc[:], bias, t[:], ADD, MAX)
 
 
 def tile_hisan_kernel(tc, table, w, b, lv_w, lv_b, cls_w, cls_b, offs, out):
     nc = tc.nc
     with (
         tc.tile_pool(name="held", bufs=1) as held,
-        tc.tile_pool(name="work", bufs=4) as work,
-        tc.psum_pool(name="warm", bufs=1) as warm,
+        tc.tile_pool(name="work", bufs=8) as work,
         tc.psum_pool(name="psum", bufs=7) as psum,
+        tc.psum_pool(name="warm", bufs=1) as warm,
     ):
         zeros = held.tile([P, P], BF16, name="zeros")
         nc.vector.memset(zeros[:], 0.0)
@@ -63,29 +61,29 @@ def tile_hisan_kernel(tc, table, w, b, lv_w, lv_b, cls_w, cls_b, offs, out):
             nc.tensor.matmul(unread[:], zeros[:], zeros[:], start=True, stop=True)
 
 
-        h1 = [held.tile([P, BLOCKS, PIECE], BF16, name=f"h1_{p}") for p in range(PIECES)]
+        h1 = [[held.tile([P, PIECE], BF16, name=f"h1_{p}_{k}") for k in range(BLOCKS)] for p in range(PIECES)]
         for p in range(PIECES):
             looked_up = table_sb[:].indirect(offsets[:, p * (PIECE // 16) : (p + 1) * (PIECE // 16)])
-            acc = psum.tile([P, BLOCKS, PIECE], F32, name="acc")
             for k in range(BLOCKS):
-                nc.tensor.matmul(acc[:, k, :], w_sb[:, k * P : (k + 1) * P], looked_up, start=True, stop=True)
-            elu_bf16(nc, work, h1[p], acc, b_sb)
+                acc = psum.tile([P, PIECE], F32, name="acc")
+                nc.tensor.matmul(acc[:], w_sb[:, k * P : (k + 1) * P], looked_up, start=True, stop=True)
+                elu_bf16(nc, work, h1[p][k], acc, b_sb[:, k : k + 1])
 
-        h2 = [held.tile([P, BLOCKS, PIECE], BF16, name=f"h2_{p}") for p in range(PIECES)]
+        h2 = [[held.tile([P, PIECE], BF16, name=f"h2_{p}_{c}") for c in range(BLOCKS)] for p in range(PIECES)]
         for p in range(PIECES):
-            acc = psum.tile([P, BLOCKS, PIECE], F32, name="acc")
             for c in range(BLOCKS):
+                acc = psum.tile([P, PIECE], F32, name="acc")
                 for k in range(BLOCKS):
                     nc.tensor.matmul(
-                        acc[:, c, :], lv_w_sb[:, k, c * P : (c + 1) * P], h1[p][:, k, :],
+                        acc[:], lv_w_sb[:, k, c * P : (c + 1) * P], h1[p][k][:],
                         start=(k == 0), stop=(k == BLOCKS - 1),
                     )
-            elu_bf16(nc, work, h2[p], acc, lv_b_sb)
+                elu_bf16(nc, work, h2[p][c], acc, lv_b_sb[:, c : c + 1])
 
         for p in range(PIECES):
             acc = psum.tile([P, PIECE], F32, name="acc")
             for c in range(BLOCKS):
-                nc.tensor.matmul(acc[:], cls_w_sb[:, c, :], h2[p][:, c, :], start=(c == 0), stop=(c == BLOCKS - 1))
+                nc.tensor.matmul(acc[:], cls_w_sb[:, c, :], h2[p][c][:], start=(c == 0), stop=(c == BLOCKS - 1))
             logits = work.tile([P, PIECE], F32, name="logits")
             nc.scalar.activation(logits[:], acc[:], IDENTITY, bias=cls_b_sb[:, 0:1])
             nc.sync.dma_start(out[:, p * PIECE : (p + 1) * PIECE], logits[:])

@@ -11,30 +11,27 @@ BLOCKS = A // P
 N = 512
 PIECE = 128
 PIECES = N // PIECE
-WARM_MATMULS = 14
 
 FLOPS = 2 * N * (P * A + A * A + A * P)
 
 
-def elu_bf16(nc, work, h, acc, bias):
-    e = work.tile([P, PIECE], F32, name="e")
-    nc.scalar.activation(e[:], acc[:], EXP, bias=bias)
-    t = work.tile([P, PIECE], F32, name="t")
+def elu_bf16(nc, work, h, accs, bias):
+    e = work.tile([P, BLOCKS, PIECE], F32, name="e")
+    for k in range(BLOCKS):
+        nc.scalar.activation(e[:, k, :], accs[k][:], EXP, bias=bias[:, k : k + 1])
+    t = work.tile([P, BLOCKS, PIECE], F32, name="t")
     nc.vector.tensor_scalar(t[:], e[:], -1.0, 0.0, ADD, MIN)
-    nc.vector.scalar_tensor_tensor(h[:], acc[:], bias, t[:], ADD, MAX)
+    for k in range(BLOCKS):
+        nc.vector.scalar_tensor_tensor(h[:, k, :], accs[k][:], bias[:, k : k + 1], t[:, k, :], ADD, MAX)
 
 
 def tile_hisan_kernel(tc, table, w, b, lv_w, lv_b, cls_w, cls_b, offs, out):
     nc = tc.nc
     with (
         tc.tile_pool(name="held", bufs=1) as held,
-        tc.tile_pool(name="work", bufs=8) as work,
-        tc.psum_pool(name="psum", bufs=7) as psum,
-        tc.psum_pool(name="warm", bufs=1) as warm,
+        tc.tile_pool(name="work", bufs=4) as work,
+        tc.psum_pool(name="psum", bufs=8) as psum,
     ):
-        zeros = held.tile([P, P], BF16, name="zeros")
-        nc.vector.memset(zeros[:], 0.0)
-
         offsets = held.tile([P, N // 16], U16, name="offsets")
         table_sb = held.tile([P, V], BF16, name="table_sb")
         w_sb = held.tile([P, A], BF16, name="w_sb")
@@ -53,37 +50,35 @@ def tile_hisan_kernel(tc, table, w, b, lv_w, lv_b, cls_w, cls_b, offs, out):
             nc.sync.dma_start(cls_w_sb[:], cls_w.rearrange("(k p) m -> p k m", p=P))
             nc.sync.dma_start(cls_b_sb[:], cls_b)
 
+        zero = held.tile([P, 1], F32, name="zero")
+        nc.vector.memset(zero[:], 0.0)
         one = held.tile([P, 1], F32, name="one")
-        nc.scalar.activation(one[:], zeros[:, 0:1], EXP)
-
-        unread = warm.tile([P, P], F32, name="unread")
-        for i in range(WARM_MATMULS):
-            nc.tensor.matmul(unread[:], zeros[:], zeros[:], start=True, stop=True)
+        nc.scalar.activation(one[:], zero[:], EXP)
 
 
-        h1 = [[held.tile([P, PIECE], BF16, name=f"h1_{p}_{k}") for k in range(BLOCKS)] for p in range(PIECES)]
+        h1 = [held.tile([P, BLOCKS, PIECE], BF16, name=f"h1_{p}") for p in range(PIECES)]
         for p in range(PIECES):
             looked_up = table_sb[:].indirect(offsets[:, p * (PIECE // 16) : (p + 1) * (PIECE // 16)])
+            accs = [psum.tile([P, PIECE], F32, name="acc") for k in range(BLOCKS)]
             for k in range(BLOCKS):
-                acc = psum.tile([P, PIECE], F32, name="acc")
-                nc.tensor.matmul(acc[:], w_sb[:, k * P : (k + 1) * P], looked_up, start=True, stop=True)
-                elu_bf16(nc, work, h1[p][k], acc, b_sb[:, k : k + 1])
+                nc.tensor.matmul(accs[k][:], w_sb[:, k * P : (k + 1) * P], looked_up, start=True, stop=True)
+            elu_bf16(nc, work, h1[p], accs, b_sb)
 
-        h2 = [[held.tile([P, PIECE], BF16, name=f"h2_{p}_{c}") for c in range(BLOCKS)] for p in range(PIECES)]
+        h2 = [held.tile([P, BLOCKS, PIECE], BF16, name=f"h2_{p}") for p in range(PIECES)]
         for p in range(PIECES):
+            accs = [psum.tile([P, PIECE], F32, name="acc") for c in range(BLOCKS)]
             for c in range(BLOCKS):
-                acc = psum.tile([P, PIECE], F32, name="acc")
                 for k in range(BLOCKS):
                     nc.tensor.matmul(
-                        acc[:], lv_w_sb[:, k, c * P : (c + 1) * P], h1[p][k][:],
+                        accs[c][:], lv_w_sb[:, k, c * P : (c + 1) * P], h1[p][:, k, :],
                         start=(k == 0), stop=(k == BLOCKS - 1),
                     )
-                elu_bf16(nc, work, h2[p][c], acc, lv_b_sb[:, c : c + 1])
+            elu_bf16(nc, work, h2[p], accs, lv_b_sb)
 
         for p in range(PIECES):
             acc = psum.tile([P, PIECE], F32, name="acc")
             for c in range(BLOCKS):
-                nc.tensor.matmul(acc[:], cls_w_sb[:, c, :], h2[p][c][:], start=(c == 0), stop=(c == BLOCKS - 1))
+                nc.tensor.matmul(acc[:], cls_w_sb[:, c, :], h2[p][:, c, :], start=(c == 0), stop=(c == BLOCKS - 1))
             logits = work.tile([P, PIECE], F32, name="logits")
             nc.scalar.activation(logits[:], acc[:], IDENTITY, bias=cls_b_sb[:, 0:1])
             nc.sync.dma_start(out[:, p * PIECE : (p + 1) * PIECE], logits[:])

@@ -41,9 +41,9 @@ def tile_hisan_kernel(tc, table, w, b, lv_w, lv_b, cls_w, cls_b, offs, out):
         cls_w_sb = held.tile([P, BLOCKS, P], BF16, name="cls_w_sb")
         cls_b_sb = held.tile([P, 1], F32, name="cls_b_sb")
         with nc.allow_non_contiguous_dma(reason="a bias goes one element to a partition"):
-            nc.sync.dma_start(offsets[:], offs)
             nc.sync.dma_start(table_sb[:], table)
             nc.scalar.dma_start(w_sb[:], w)
+            nc.sync.dma_start(offsets[:], offs)
             nc.scalar.dma_start(b_sb[:], b.rearrange("(k p) o -> p (k o)", p=P))
             nc.sync.dma_start(lv_w_sb[:], lv_w.rearrange("(k p) c -> p k c", p=P))
             nc.sync.dma_start(lv_b_sb[:], lv_b.rearrange("(k p) o -> p (k o)", p=P))

@@ -2,7 +2,11 @@ import concourse.mybir as mybir
 
 BF16, F32, U16 = mybir.dt.bfloat16, mybir.dt.float32, mybir.dt.uint16
 ADD, MIN, MAX = mybir.AluOpType.add, mybir.AluOpType.min, mybir.AluOpType.max
-EXP, IDENTITY = mybir.ActivationFunctionType.Exp, mybir.ActivationFunctionType.Identity
+EXP, RELU, IDENTITY = (
+    mybir.ActivationFunctionType.Exp,
+    mybir.ActivationFunctionType.Relu,
+    mybir.ActivationFunctionType.Identity,
+)
 
 P = 128
 V = 256
@@ -19,10 +23,12 @@ def elu_bf16(nc, work, h, accs, bias):
     e = work.tile([P, BLOCKS, PIECE], F32, name="e")
     for k in range(BLOCKS):
         nc.scalar.activation(e[:, k, :], accs[k][:], EXP, bias=bias[:, k : k + 1])
-    t = work.tile([P, BLOCKS, PIECE], F32, name="t")
-    nc.vector.tensor_scalar(t[:], e[:], -1.0, 0.0, ADD, MIN)
-    for k in range(BLOCKS):
-        nc.vector.scalar_tensor_tensor(h[:, k, :], accs[k][:], bias[:, k : k + 1], t[:, k, :], ADD, MAX)
+    r = work.tile([P, PIECE], F32, name="r")
+    nc.scalar.activation(r[:], accs[1][:], RELU, bias=bias[:, 1:2])
+    t = work.tile([P, PIECE], F32, name="t")
+    nc.vector.tensor_scalar(t[:], e[:, 0, :], -1.0, 0.0, ADD, MIN)
+    nc.vector.scalar_tensor_tensor(h[:, 0, :], accs[0][:], bias[:, 0:1], t[:], ADD, MAX)
+    nc.vector.scalar_tensor_tensor(h[:, 1, :], e[:, 1, :], -1.0, r[:], ADD, MIN)
 
 
 def tile_hisan_kernel(tc, table, w, b, lv_w, lv_b, cls_w, cls_b, offs, out):

@@ -19,16 +19,23 @@ PIECES = N // PIECE
 FLOPS = 2 * N * (P * A + A * A + A * P)
 
 
-def elu_bf16(nc, work, h, accs, bias):
+def elu_bf16(nc, work, h, accs, bias, relu_blocks):
     e = work.tile([P, BLOCKS, PIECE], F32, name="e")
     for k in range(BLOCKS):
         nc.scalar.activation(e[:, k, :], accs[k][:], EXP, bias=bias[:, k : k + 1])
-    r = work.tile([P, PIECE], F32, name="r")
-    nc.scalar.activation(r[:], accs[1][:], RELU, bias=bias[:, 1:2])
-    t = work.tile([P, PIECE], F32, name="t")
-    nc.vector.tensor_scalar(t[:], e[:, 0, :], -1.0, 0.0, ADD, MIN)
-    nc.vector.scalar_tensor_tensor(h[:, 0, :], accs[0][:], bias[:, 0:1], t[:], ADD, MAX)
-    nc.vector.scalar_tensor_tensor(h[:, 1, :], e[:, 1, :], -1.0, r[:], ADD, MIN)
+    other = work.tile([P, BLOCKS, PIECE], F32, name="other")
+    for k in relu_blocks:
+        nc.scalar.activation(other[:, k, :], accs[k][:], RELU, bias=bias[:, k : k + 1])
+    for k in range(BLOCKS):
+        if k in relu_blocks:
+            nc.vector.scalar_tensor_tensor(h[:, k, :], e[:, k, :], -1.0, other[:, k, :], ADD, MIN)
+        else:
+            nc.vector.tensor_scalar(other[:, k, :], e[:, k, :], -1.0, 0.0, ADD, MIN)
+            nc.vector.scalar_tensor_tensor(h[:, k, :], accs[k][:], bias[:, k : k + 1], other[:, k, :], ADD, MAX)
+
+
+def relu_blocks_of(p):
+    return (1,) if p % 2 == 1 else ()
 
 
 def tile_hisan_kernel(tc, table, w, b, lv_w, lv_b, cls_w, cls_b, offs, out):
@@ -68,7 +75,7 @@ def tile_hisan_kernel(tc, table, w, b, lv_w, lv_b, cls_w, cls_b, offs, out):
             accs = [psum.tile([P, PIECE], F32, name="acc") for k in range(BLOCKS)]
             for k in range(BLOCKS):
                 nc.tensor.matmul(accs[k][:], w_sb[:, k * P : (k + 1) * P], looked_up, start=True, stop=True)
-            elu_bf16(nc, work, h1[p], accs, b_sb)
+            elu_bf16(nc, work, h1[p], accs, b_sb, relu_blocks_of(p))
 
         h2 = [held.tile([P, BLOCKS, PIECE], BF16, name=f"h2_{p}") for p in range(PIECES)]
         for p in range(PIECES):
@@ -79,7 +86,7 @@ def tile_hisan_kernel(tc, table, w, b, lv_w, lv_b, cls_w, cls_b, offs, out):
                         accs[c][:], lv_w_sb[:, k, c * P : (c + 1) * P], h1[p][:, k, :],
                         start=(k == 0), stop=(k == BLOCKS - 1),
                     )
-            elu_bf16(nc, work, h2[p], accs, lv_b_sb)
+            elu_bf16(nc, work, h2[p], accs, lv_b_sb, relu_blocks_of(p))
 
         for p in range(PIECES):
             acc = psum.tile([P, PIECE], F32, name="acc")

@@ -34,6 +34,23 @@ def elu_bf16(nc, work, h, accs, bias, relu_blocks):
             nc.vector.scalar_tensor_tensor(h[:, k, :], accs[k][:], bias[:, k : k + 1], other[:, k, :], ADD, MAX)
 
 
+POSITIVE, NEGATIVE = 0, 1
+TERMS = 2
+
+
+def elu_terms(nc, work, h, accs, bias, relu_blocks):
+    e = work.tile([P, BLOCKS, PIECE], F32, name="e")
+    for k in range(BLOCKS):
+        nc.scalar.activation(e[:, k, :], accs[k][:], EXP, bias=bias[:, k : k + 1])
+    for k in range(BLOCKS):
+        nc.vector.tensor_scalar(h[:, k, NEGATIVE, :], e[:, k, :], -1.0, 0.0, ADD, MIN)
+    for k in range(BLOCKS):
+        if k in relu_blocks:
+            nc.scalar.activation(h[:, k, POSITIVE, :], accs[k][:], RELU, bias=bias[:, k : k + 1])
+        else:
+            nc.vector.tensor_scalar(h[:, k, POSITIVE, :], accs[k][:], bias[:, k : k + 1], 0.0, ADD, MAX)
+
+
 def relu_blocks_of(p):
     return (1,) if p % 2 == 1 else ()
 
@@ -77,7 +94,7 @@ def tile_hisan_kernel(tc, table, w, b, lv_w, lv_b, cls_w, cls_b, offs, out):
                 nc.tensor.matmul(accs[k][:], w_sb[:, k * P : (k + 1) * P], looked_up, start=True, stop=True)
             elu_bf16(nc, work, h1[p], accs, b_sb, relu_blocks_of(p))
 
-        h2 = [held.tile([P, BLOCKS, PIECE], BF16, name=f"h2_{p}") for p in range(PIECES)]
+        h2 = [held.tile([P, BLOCKS, TERMS, PIECE], BF16, name=f"h2_{p}") for p in range(PIECES)]
         for p in range(PIECES):
             accs = [psum.tile([P, PIECE], F32, name="acc") for c in range(BLOCKS)]
             for c in range(BLOCKS):
@@ -86,12 +103,16 @@ def tile_hisan_kernel(tc, table, w, b, lv_w, lv_b, cls_w, cls_b, offs, out):
                         accs[c][:], lv_w_sb[:, k, c * P : (c + 1) * P], h1[p][:, k, :],
                         start=(k == 0), stop=(k == BLOCKS - 1),
                     )
-            elu_bf16(nc, work, h2[p], accs, lv_b_sb, relu_blocks_of(p))
+            elu_terms(nc, work, h2[p], accs, lv_b_sb, relu_blocks_of(p))
 
         for p in range(PIECES):
             acc = psum.tile([P, PIECE], F32, name="acc")
-            for c in range(BLOCKS):
-                nc.tensor.matmul(acc[:], cls_w_sb[:, c, :], h2[p][:, c, :], start=(c == 0), stop=(c == BLOCKS - 1))
+            steps = [(c, term) for term in (NEGATIVE, POSITIVE) for c in range(BLOCKS)]
+            for c, term in steps:
+                nc.tensor.matmul(
+                    acc[:], cls_w_sb[:, c, :], h2[p][:, c, term, :],
+                    start=((c, term) == steps[0]), stop=((c, term) == steps[-1]),
+                )
             logits = work.tile([P, PIECE], F32, name="logits")
             nc.scalar.activation(logits[:], acc[:], IDENTITY, bias=cls_b_sb[:, 0:1])
             nc.sync.dma_start(out[:, p * PIECE : (p + 1) * PIECE], logits[:])

@@ -38,12 +38,15 @@ POSITIVE, NEGATIVE = 0, 1
 TERMS = 2
 
 
-def elu_terms(nc, work, h, accs, bias, relu_blocks):
+def elu_terms(nc, work, h, accs, bias, relu_blocks, last):
     e = work.tile([P, BLOCKS, PIECE], F32, name="e")
     for k in range(BLOCKS):
         nc.scalar.activation(e[:, k, :], accs[k][:], EXP, bias=bias[:, k : k + 1])
-    for k in range(BLOCKS):
-        nc.vector.tensor_scalar(h[:, k, NEGATIVE, :], e[:, k, :], -1.0, 0.0, ADD, MIN)
+    if last:
+        for k in range(BLOCKS):
+            nc.vector.tensor_scalar(h[:, k, NEGATIVE, :], e[:, k, :], -1.0, 0.0, ADD, MIN)
+    else:
+        nc.vector.tensor_scalar(h[:, :, NEGATIVE, :], e[:], -1.0, 0.0, ADD, MIN)
     for k in range(BLOCKS):
         if k in relu_blocks:
             nc.scalar.activation(h[:, k, POSITIVE, :], accs[k][:], RELU, bias=bias[:, k : k + 1])
@@ -103,7 +106,8 @@ def tile_hisan_kernel(tc, table, w, b, lv_w, lv_b, cls_w, cls_b, offs, out):
                         accs[c][:], lv_w_sb[:, k, c * P : (c + 1) * P], h1[p][:, k, :],
                         start=(k == 0), stop=(k == BLOCKS - 1),
                     )
-            elu_terms(nc, work, h2[p], accs, lv_b_sb, relu_blocks_of(p))
+            last = p == PIECES - 1
+            elu_terms(nc, work, h2[p], accs, lv_b_sb, range(BLOCKS) if last else relu_blocks_of(p), last)
 
         for p in range(PIECES):
             acc = psum.tile([P, PIECE], F32, name="acc")
@@ -114,5 +118,8 @@ def tile_hisan_kernel(tc, table, w, b, lv_w, lv_b, cls_w, cls_b, offs, out):
                     start=((c, term) == steps[0]), stop=((c, term) == steps[-1]),
                 )
             logits = work.tile([P, PIECE], F32, name="logits")
-            nc.scalar.activation(logits[:], acc[:], IDENTITY, bias=cls_b_sb[:, 0:1])
+            if p < PIECES - 1:
+                nc.scalar.activation(logits[:], acc[:], IDENTITY, bias=cls_b_sb[:, 0:1])
+            else:
+                nc.vector.tensor_scalar_add(logits[:], acc[:], cls_b_sb[:, 0:1])
             nc.sync.dma_start(out[:, p * PIECE : (p + 1) * PIECE], logits[:])

@@ -77,10 +77,10 @@ def tile_hisan_kernel(tc, table, w, b, lv_w, lv_b, cls_w, cls_b, offs, out):
             nc.sync.dma_start(table_sb[:], table)
             nc.scalar.dma_start(w_sb[:], w)
             nc.sync.dma_start(offsets[:], offs)
-            nc.scalar.dma_start(b_sb[:], b.rearrange("(k p) o -> p (k o)", p=P))
-            nc.sync.dma_start(lv_w_sb[:], lv_w.rearrange("(k p) c -> p k c", p=P))
-            nc.sync.dma_start(lv_b_sb[:], lv_b.rearrange("(k p) o -> p (k o)", p=P))
-            nc.sync.dma_start(cls_w_sb[:], cls_w.rearrange("(k p) m -> p k m", p=P))
+            nc.scalar.dma_start(b_sb[:], b.rearrange("(p k) o -> p (k o)", p=P))
+            nc.sync.dma_start(lv_w_sb[:], lv_w.rearrange("(p k) c -> p k c", p=P))
+            nc.sync.dma_start(lv_b_sb[:], lv_b.rearrange("(p k) o -> p (k o)", p=P))
+            nc.sync.dma_start(cls_w_sb[:], cls_w.rearrange("(p k) m -> p k m", p=P))
             nc.sync.dma_start(cls_b_sb[:], cls_b)
 
         zero = held.tile([P, 1], F32, name="zero")
@@ -94,7 +94,7 @@ def tile_hisan_kernel(tc, table, w, b, lv_w, lv_b, cls_w, cls_b, offs, out):
             looked_up = table_sb[:].indirect(offsets[:, p * (PIECE // 16) : (p + 1) * (PIECE // 16)])
             accs = [psum.tile([P, PIECE], F32, name="acc") for k in range(BLOCKS)]
             for k in range(BLOCKS):
-                nc.tensor.matmul(accs[k][:], w_sb[:, k * P : (k + 1) * P], looked_up, start=True, stop=True)
+                nc.tensor.matmul(accs[k][:], w_sb[:, k::BLOCKS], looked_up, start=True, stop=True)
             elu_bf16(nc, work, h1[p], accs, b_sb, relu_blocks_of(p))
 
         h2 = [held.tile([P, BLOCKS, TERMS, PIECE], BF16, name=f"h2_{p}") for p in range(PIECES)]
@@ -103,7 +103,7 @@ def tile_hisan_kernel(tc, table, w, b, lv_w, lv_b, cls_w, cls_b, offs, out):
             for c in range(BLOCKS):
                 for k in range(BLOCKS):
                     nc.tensor.matmul(
-                        accs[c][:], lv_w_sb[:, k, c * P : (c + 1) * P], h1[p][:, k, :],
+                        accs[c][:], lv_w_sb[:, k, c::BLOCKS], h1[p][:, k, :],
                         start=(k == 0), stop=(k == BLOCKS - 1),
                     )
             last = p == PIECES - 1

@@ -111,7 +111,10 @@ def tile_hisan_kernel(tc, table, w, b, lv_w, lv_b, cls_w, cls_b, offs, out):
 
         for p in range(PIECES):
             acc = psum.tile([P, PIECE], F32, name="acc")
-            steps = [(c, term) for term in (NEGATIVE, POSITIVE) for c in range(BLOCKS)]
+            if p < PIECES - 1:
+                steps = [(0, POSITIVE), (0, NEGATIVE), (1, NEGATIVE), (1, POSITIVE)]
+            else:
+                steps = [(0, POSITIVE), (1, POSITIVE), (0, NEGATIVE), (1, NEGATIVE)]
             for c, term in steps:
                 nc.tensor.matmul(
                     acc[:], cls_w_sb[:, c, :], h2[p][:, c, term, :],

import concourse.mybir as mybir

BF16, F32, U16 = mybir.dt.bfloat16, mybir.dt.float32, mybir.dt.uint16
ADD, MIN, MAX = mybir.AluOpType.add, mybir.AluOpType.min, mybir.AluOpType.max
EXP, RELU, IDENTITY = (
    mybir.ActivationFunctionType.Exp,
    mybir.ActivationFunctionType.Relu,
    mybir.ActivationFunctionType.Identity,
)

P = 128
V = 256
A = 256
BLOCKS = A // P
N = 512
PIECE = 128
PIECES = N // PIECE

FLOPS = 2 * N * (P * A + A * A + A * P)


def elu_bf16(nc, work, h, accs, bias, relu_blocks):
    e = work.tile([P, BLOCKS, PIECE], F32, name="e")
    for k in range(BLOCKS):
        nc.scalar.activation(e[:, k, :], accs[k][:], EXP, bias=bias[:, k : k + 1])
    other = work.tile([P, BLOCKS, PIECE], F32, name="other")
    for k in relu_blocks:
        nc.scalar.activation(other[:, k, :], accs[k][:], RELU, bias=bias[:, k : k + 1])
    for k in range(BLOCKS):
        if k in relu_blocks:
            nc.vector.scalar_tensor_tensor(h[:, k, :], e[:, k, :], -1.0, other[:, k, :], ADD, MIN)
        else:
            nc.vector.tensor_scalar(other[:, k, :], e[:, k, :], -1.0, 0.0, ADD, MIN)
            nc.vector.scalar_tensor_tensor(h[:, k, :], accs[k][:], bias[:, k : k + 1], other[:, k, :], ADD, MAX)


POSITIVE, NEGATIVE = 0, 1
TERMS = 2


def elu_terms(nc, work, h, accs, bias, relu_blocks, last):
    e = work.tile([P, BLOCKS, PIECE], F32, name="e")
    for k in range(BLOCKS):
        nc.scalar.activation(e[:, k, :], accs[k][:], EXP, bias=bias[:, k : k + 1])
    if last:
        for k in range(BLOCKS):
            nc.vector.tensor_scalar(h[:, k, NEGATIVE, :], e[:, k, :], -1.0, 0.0, ADD, MIN)
    else:
        nc.vector.tensor_scalar(h[:, :, NEGATIVE, :], e[:], -1.0, 0.0, ADD, MIN)
    for k in range(BLOCKS):
        if k in relu_blocks:
            nc.scalar.activation(h[:, k, POSITIVE, :], accs[k][:], RELU, bias=bias[:, k : k + 1])
        else:
            nc.vector.tensor_scalar(h[:, k, POSITIVE, :], accs[k][:], bias[:, k : k + 1], 0.0, ADD, MAX)


def relu_blocks_of(p):
    return (1,) if p % 2 == 1 else ()


def tile_hisan_kernel(tc, table, w, b, lv_w, lv_b, cls_w, cls_b, offs, out):
    nc = tc.nc
    with (
        tc.tile_pool(name="held", bufs=1) as held,
        tc.tile_pool(name="work", bufs=4) as work,
        tc.psum_pool(name="psum", bufs=8) as psum,
    ):
        offsets = held.tile([P, N // 16], U16, name="offsets")
        table_sb = held.tile([P, V], BF16, name="table_sb")
        w_sb = held.tile([P, A], BF16, name="w_sb")
        b_sb = held.tile([P, BLOCKS], F32, name="b_sb")
        lv_w_sb = held.tile([P, BLOCKS, A], BF16, name="lv_w_sb")
        lv_b_sb = held.tile([P, BLOCKS], F32, name="lv_b_sb")
        cls_w_sb = held.tile([P, BLOCKS, P], BF16, name="cls_w_sb")
        cls_b_sb = held.tile([P, 1], F32, name="cls_b_sb")
        with nc.allow_non_contiguous_dma(reason="a bias goes one element to a partition"):
            nc.sync.dma_start(table_sb[:], table)
            nc.scalar.dma_start(w_sb[:], w)
            nc.sync.dma_start(offsets[:], offs)
            nc.scalar.dma_start(b_sb[:], b.rearrange("(p k) o -> p (k o)", p=P))
            nc.sync.dma_start(lv_w_sb[:], lv_w.rearrange("(p k) c -> p k c", p=P))
            nc.sync.dma_start(lv_b_sb[:], lv_b.rearrange("(p k) o -> p (k o)", p=P))
            nc.sync.dma_start(cls_w_sb[:], cls_w.rearrange("(p k) m -> p k m", p=P))
            nc.sync.dma_start(cls_b_sb[:], cls_b)

        zero = held.tile([P, 1], F32, name="zero")
        nc.vector.memset(zero[:], 0.0)
        one = held.tile([P, 1], F32, name="one")
        nc.scalar.activation(one[:], zero[:], EXP)


        h1 = [held.tile([P, BLOCKS, PIECE], BF16, name=f"h1_{p}") for p in range(PIECES)]
        for p in range(PIECES):
            looked_up = table_sb[:].indirect(offsets[:, p * (PIECE // 16) : (p + 1) * (PIECE // 16)])
            accs = [psum.tile([P, PIECE], F32, name="acc") for k in range(BLOCKS)]
            for k in range(BLOCKS):
                nc.tensor.matmul(accs[k][:], w_sb[:, k::BLOCKS], looked_up, start=True, stop=True)
            elu_bf16(nc, work, h1[p], accs, b_sb, relu_blocks_of(p))

        h2 = [held.tile([P, BLOCKS, TERMS, PIECE], BF16, name=f"h2_{p}") for p in range(PIECES)]
        for p in range(PIECES):
            accs = [psum.tile([P, PIECE], F32, name="acc") for c in range(BLOCKS)]
            for c in range(BLOCKS):
                for k in range(BLOCKS):
                    nc.tensor.matmul(
                        accs[c][:], lv_w_sb[:, k, c::BLOCKS], h1[p][:, k, :],
                        start=(k == 0), stop=(k == BLOCKS - 1),
                    )
            last = p == PIECES - 1
            elu_terms(nc, work, h2[p], accs, lv_b_sb, range(BLOCKS) if last else relu_blocks_of(p), last)

        for p in range(PIECES):
            acc = psum.tile([P, PIECE], F32, name="acc")
            if p < PIECES - 1:
                steps = [(0, POSITIVE), (0, NEGATIVE), (1, NEGATIVE), (1, POSITIVE)]
            else:
                steps = [(0, POSITIVE), (1, POSITIVE), (0, NEGATIVE), (1, NEGATIVE)]
            for c, term in steps:
                nc.tensor.matmul(
                    acc[:], cls_w_sb[:, c, :], h2[p][:, c, term, :],
                    start=((c, term) == steps[0]), stop=((c, term) == steps[-1]),
                )
            logits = work.tile([P, PIECE], F32, name="logits")
            if p < PIECES - 1:
                nc.scalar.activation(logits[:], acc[:], IDENTITY, bias=cls_b_sb[:, 0:1])
            else:
                nc.vector.tensor_scalar_add(logits[:], acc[:], cls_b_sb[:, 0:1])
            nc.sync.dma_start(out[:, p * PIECE : (p + 1) * PIECE], logits[:])
